import numpy as np
import ml_dtypes


def mxq(x, axis, fmt="e4m3"):
    dtype, down = {"e4m3": (ml_dtypes.float8_e4m3fn, 7), "e5m2": (ml_dtypes.float8_e5m2, 14)}[fmt]
    v = np.moveaxis(np.asarray(x, np.float32).astype(ml_dtypes.bfloat16).astype(np.float64), axis, -1)
    blocks = v.reshape(v.shape[:-1] + (-1, 32))
    amax = np.abs(blocks).max(-1, keepdims=True)
    byte = np.maximum(np.where(amax > 0, np.frexp(amax)[1] - 1 + 127, 0) - down, 1)
    scale = np.exp2(byte - 127.0)
    codes = (blocks / scale).astype(np.float32).astype(dtype).astype(np.float64)
    return np.moveaxis((codes * scale).reshape(v.shape), -1, axis)


WIDE = False


def mx_kscale(k):
    if not WIDE:
        return np.ones(k)
    levels = np.array([10, -10, 5, -5, 0])
    if k % 512:
        return np.exp2(np.random.permutation(np.resize(levels, k // 32))).repeat(32)
    a = np.empty((k // 512, 16))
    for p in range(k // 512):
        a[p, :8] = np.random.permutation(np.resize(levels, 8))
        for g in range(8):
            far = levels[np.abs(levels - a[p, g]) >= 10]
            a[p, g + 8] = far[np.random.randint(len(far))]
    return np.exp2(a.ravel()).repeat(32)


BF16 = ml_dtypes.bfloat16


def bf(x):
    return np.asarray(x, np.float32).astype(BF16)


def f64(x):
    return np.asarray(x).astype(np.float64)


B, D, U = 2048, 512, 128


def sigmoid(v):
    return 1.0 / (1.0 + np.exp(-v))


def setup_inputs():
    s = mx_kscale(D)
    inp = {"pre_layer": bf(np.random.standard_normal((2, B, U))), "x": bf(np.random.standard_normal((B, D)) * s)}
    for n in ("W_i", "W_f", "W_o", "W_c"):
        inp[n] = bf(np.random.standard_normal((D, U)) / np.sqrt(D) / s[:, None])
    for n in ("U_i", "U_f", "U_o", "U_c"):
        inp[n] = bf(np.random.standard_normal((U, U)) / np.sqrt(U))
    return inp


def reference(pre_layer, x, W_i, W_f, W_o, W_c, U_i, U_f, U_o, U_c):
    pre = f64(pre_layer)
    pre_h, pre_c = pre[0], pre[1]
    W = np.concatenate([f64(W_i), f64(W_f), f64(W_o), f64(W_c)], axis=1)
    Uw = np.concatenate([f64(U_i), f64(U_f), f64(U_o), f64(U_c)], axis=1)
    gates = (mxq(f64(x), 1, "e4m3") @ mxq(W, 0, "e4m3")) + pre_h @ Uw
    zi, zf, zo, zc = np.split(gates, 4, axis=1)
    i_t = sigmoid(zi)
    f_t = sigmoid(zf)
    o_t = sigmoid(zo)
    n_c_t = np.tanh(zc)
    c = f_t * pre_c + i_t * n_c_t
    h = o_t * np.tanh(c)
    return np.stack([h, c])

@@ -1,0 +1,291 @@
+from contextlib import ExitStack
+
+import concourse.mybir as mybir
+from concourse.masks import make_identity
+
+FLOPS = 2 * 2048 * 512 * 512 + 2 * 2048 * 128 * 512
+
+F32 = mybir.dt.float32
+BF16 = mybir.dt.bfloat16
+U32 = mybir.dt.uint32
+U8 = mybir.dt.uint8
+FP8X4 = mybir.dt.float8_e4m3fn_x4
+ACT = mybir.ActivationFunctionType
+ALU = mybir.AluOpType
+
+P = 128
+NT = 16
+NP = NT // 2
+D = 512
+U = 128
+G4 = 4 * U
+
+MX_AHEAD = 2
+FRONT_FIRST = 3
+FRONT_STEP = 2
+H1_AT = 2
+G_PAIRS = 5
+S_COPIES = 5
+V_ADD = (1,)
+
+
+def tile_lstm_kernel(tc, pre_layer, x, W_i, W_f, W_o, W_c, U_i, U_f, U_o, U_c, out):
+    nc = tc.nc
+    with ExitStack() as ctx:
+        keep = ctx.enter_context(tc.tile_pool(name="keep", bufs=1))
+        work = ctx.enter_context(tc.tile_pool(name="work", bufs=5))
+        psum = ctx.enter_context(tc.psum_pool(name="psum", bufs=2))
+        ctx.enter_context(tc.manual_schedule())
+
+        xv = x.rearrange("(p t) k -> p t k", t=NT)
+        prev = pre_layer.rearrange("s (p t) u -> s p t u", t=NT)
+        outv = out.rearrange("s (p t) u -> s p t u", t=NT)
+
+        x_sb = [keep.tile([P, 2 * D], BF16, name="x%d" % k) for k in range(NP)]
+        w_raw = [keep.tile([P, 4 * U], BF16, name="w_raw%d" % g) for g in range(4)]
+        u_sb = keep.tile([P, G4], BF16, name="u_sb")
+        ph_sb = [keep.tile([P, 8, U], BF16, name="ph%d" % i) for i in range(2)]
+        pc_sb = keep.tile([P, NT, U], BF16, name="pc_sb")
+
+        def load_x(k):
+            nc.sync.dma_start(
+                out=x_sb[k][:].rearrange("p (t k) -> p t k", t=2), in_=xv[:, 2 * k : 2 * k + 2, :]
+            )
+
+        load_x(0)
+        nc.scalar.dma_start(out=ph_sb[0][:], in_=prev[0, :, 0:8, :])
+        for g, w in enumerate((W_i, W_f, W_o, W_c)):
+            nc.sync.dma_start(
+                out=w_raw[g][:],
+                in_=w.rearrange("(q e) c -> q (e c)", e=4),
+            )
+        for g, uw in enumerate((U_i, U_f, U_o, U_c)):
+            nc.scalar.dma_start(out=u_sb[:, g * U : (g + 1) * U], in_=uw)
+        for k in (1, 2, 3, 4, 5):
+            load_x(k)
+        nc.sync.dma_start(out=pc_sb[:], in_=prev[1])
+        load_x(6)
+        load_x(7)
+        nc.sync.dma_start(out=ph_sb[1][:], in_=prev[0, :, 8:16, :])
+
+        ident_f = keep.tile([P, P], F32, name="ident_f")
+        make_identity(nc, ident_f[:])
+        ident_b = keep.tile([P, P], BF16, name="ident_b")
+        make_identity(nc, ident_b[:])
+        warm = keep.tile([P, 1], F32, name="warm")
+        nc.vector.memset(warm[:], 0.0)
+        warm2 = keep.tile([P, 1], F32, name="warm2")
+        nc.scalar.activation(out=warm2[:], in_=warm[:], func=ACT.Sigmoid)
+
+        wg = keep.tile([P, 4 * G4], BF16, name="wg", align_bytes=64)
+        wq = keep.tile([P, G4], U32, name="wq", align_bytes=64)
+        ws = keep.tile([P, G4], U8, name="ws", align_bytes=64)
+        xq = keep.tile([P, NT * P], U32, name="xq", align_bytes=64)
+        xs = keep.tile([P, NT * P], U8, name="xs", align_bytes=64)
+        hT_sb = [keep.tile([P, 8 * P], BF16, name="hT%d" % i) for i in range(2)]
+
+        def w_regroup(g):
+            nc.vector.tensor_copy(
+                out=wg[:, g * 4 * U : (g + 1) * 4 * U].rearrange("p (c t) -> p c t", t=4),
+                in_=w_raw[g][:].rearrange("p (t c) -> p c t", t=4),
+            )
+
+        def w_quant(g):
+            nc.vector.quantize_mx(
+                out=wq[:, g * U : (g + 1) * U].bitcast(FP8X4),
+                scales=ws[:, g * U : (g + 1) * U],
+                in_=wg[:, g * 4 * U : (g + 1) * 4 * U],
+            )
+
+        xg_of = {}
+
+        def x_front(k):
+            xt = psum.tile([P, 2, 2, P], F32, name="xt", tag="tz", bufs=4)
+            xw = x_sb[k][:].bitcast(F32)
+            for j in range(2):
+                for u in range(2):
+                    words = xw[:, j * (D // 2) + u : (j + 1) * (D // 2) : 2]
+                    nc.tensor.transpose(xt[:, j, u, :], words, ident_f[:])
+            xg = work.tile([P, 2 * D], BF16, name="xg", tag="xg", align_bytes=64)
+            dst = xg[:].bitcast(F32).rearrange("p (j r u) -> p j r u", j=2, r=P, u=2)
+            src = xt[:].rearrange("p j u r -> p j r u")
+            if k % 2 == 1:
+                nc.vector.tensor_copy(out=dst, in_=src)
+            else:
+                nc.scalar.copy(out=dst, in_=src)
+            xg_of[k] = xg
+
+        def x_quant(k):
+            cols = slice(2 * k * P, (2 * k + 2) * P)
+            nc.vector.quantize_mx(out=xq[:, cols].bitcast(FP8X4), scales=xs[:, cols], in_=xg_of[k][:])
+
+        def h_half(i):
+            ht = psum.tile([P, 8, P], BF16, name="ht", tag="tz", bufs=4)
+            for j in range(8):
+                nc.tensor.transpose(ht[:, j, :], ph_sb[i][:, j, :], ident_b[:])
+            nc.scalar.copy(out=hT_sb[i][:], in_=ht[:].rearrange("p j r -> p (j r)"))
+
+        mt_of = {}
+
+        z_of = {}
+
+        def mx_pair_plain_sum(k):
+            mxs = []
+            for j in range(2):
+                t = 2 * k + j
+                cols = slice(t * P, (t + 1) * P)
+                mx = psum.tile([P, G4], F32, name="mx", tag="mt", bufs=4)
+                nc.tensor.matmul_mx(
+                    out=mx[:],
+                    lhsT=xq[:, cols].bitcast(FP8X4),
+                    lhsT_scale=xs[:, cols],
+                    rhs=wq[:].bitcast(FP8X4),
+                    rhs_scale=ws[:],
+                    start=True,
+                    stop=True,
+                )
+                mxs.append(mx)
+            pps = []
+            for j in range(2):
+                t = 2 * k + j
+                pp = psum.tile([P, G4], F32, name="pp", tag="tz", bufs=4)
+                nc.tensor.matmul(
+                    out=pp[:], lhsT=hT_sb[t // 8][:, (t % 8) * P : (t % 8 + 1) * P], rhs=u_sb[:], start=True, stop=True
+                )
+                pps.append(pp)
+            z_sb = work.tile([P, 2, G4], F32, name="z_sb", tag="z_sb")
+            for j in range(2):
+                nc.scalar.copy(out=z_sb[:, j, :], in_=pps[j][:])
+            for j in range(2):
+                nc.vector.tensor_tensor(out=z_sb[:, j, :], in0=mxs[j][:], in1=z_sb[:, j, :], op=ALU.add)
+            z_of[k] = z_sb
+
+        def mx_pair(k):
+            if k in V_ADD:
+                mx_pair_plain_sum(k)
+                return
+            cols = slice(2 * k * P, (2 * k + 2) * P)
+            for b in range(2):
+                mt = psum.tile([P, 2, 2 * P], F32, name="mt", tag="mt", bufs=4)
+                for gg in range(2):
+                    g = 2 * b + gg
+                    nc.tensor.matmul_mx(
+                        out=mt[:, gg, :],
+                        lhsT=wq[:, g * U : (g + 1) * U].bitcast(FP8X4),
+                        lhsT_scale=ws[:, g * U : (g + 1) * U],
+                        rhs=xq[:, cols].bitcast(FP8X4),
+                        rhs_scale=xs[:, cols],
+                        start=True,
+                        stop=True,
+                    )
+                mt_sb = work.tile([P, 2, 2 * P], F32, name="mt_sb%d" % b, tag="mt_sb%d" % b)
+                if b == 0 or k >= S_COPIES:
+                    nc.vector.tensor_copy(out=mt_sb[:], in_=mt[:])
+                else:
+                    nc.scalar.copy(out=mt_sb[:], in_=mt[:])
+                mt_of[(k, b)] = mt_sb
+
+        a_of = {}
+
+        def gates(t):
+            k, j = t // 2, t % 2
+            if j == 0:
+                a_new = work.tile([P, 2, G4], F32, name="a", tag="a")
+                a_of[k] = a_new
+            a = a_of[k]
+            if k in V_ADD:
+                if j == 0:
+                    z_sb = z_of[k]
+                    nc.scalar.activation(out=a[:, :, 0 : 3 * U], in_=z_sb[:, :, 0 : 3 * U], func=ACT.Sigmoid)
+                    nc.scalar.activation(out=a[:, :, 3 * U : G4], in_=z_sb[:, :, 3 * U : G4], func=ACT.Tanh)
+                return
+            zt = psum.tile([P, G4], F32, name="zt", tag="tz", bufs=4)
+            nc.tensor.matmul(
+                out=zt[:], lhsT=hT_sb[t // 8][:, (t % 8) * P : (t % 8 + 1) * P], rhs=u_sb[:], start=True, stop=False
+            )
+            for g in range(4):
+                nc.tensor.matmul(
+                    out=zt[:, g * U : (g + 1) * U],
+                    lhsT=mt_of[(k, g // 2)][:, g % 2, j * P : (j + 1) * P],
+                    rhs=ident_f[:],
+                    is_transpose=True,
+                    start=False,
+                    stop=(g == 3),
+                )
+            nc.scalar.activation(out=a[:, j, 0 : 3 * U], in_=zt[:, 0 : 3 * U], func=ACT.Sigmoid)
+            nc.scalar.activation(out=a[:, j, 3 * U : G4], in_=zt[:, 3 * U : G4], func=ACT.Tanh)
+
+        tc_of = {}
+        c_of = {}
+
+        def cell(k):
+            eng = nc.gpsimd if k < G_PAIRS else nc.vector
+            a = a_of[k]
+            fa = work.tile([P, 2, U], F32, name="fa", tag="fa")
+            eng.tensor_tensor(out=fa[:], in0=a[:, :, U : 2 * U], in1=pc_sb[:, 2 * k : 2 * k + 2, :], op=ALU.mult)
+            ib = work.tile([P, 2, U], F32, name="ib", tag="ib")
+            eng.tensor_tensor(out=ib[:], in0=a[:, :, 0:U], in1=a[:, :, 3 * U : G4], op=ALU.mult)
+            c_sb = work.tile([P, 2, U], F32, name="c_sb", tag="c_sb")
+            eng.tensor_tensor(out=c_sb[:], in0=fa[:], in1=ib[:], op=ALU.add)
+            nc.sync.dma_start(out=outv[1, :, 2 * k : 2 * k + 2, :], in_=c_sb[:])
+            c_of[k] = c_sb
+
+        def cell_tanh(k):
+            tc_sb = work.tile([P, 2, U], F32, name="tc_sb", tag="tc_sb")
+            nc.scalar.activation(out=tc_sb[:], in_=c_of[k][:], func=ACT.Tanh)
+            tc_of[k] = tc_sb
+
+        def hidden(k):
+            h_sb = work.tile([P, 2, U], F32, name="h_sb", tag="h_sb")
+            nc.vector.tensor_tensor(out=h_sb[:], in0=a_of[k][:, :, 2 * U : 3 * U], in1=tc_of[k][:], op=ALU.mult)
+            nc.sync.dma_start(out=outv[0, :, 2 * k : 2 * k + 2, :], in_=h_sb[:])
+
+        for g in range(4):
+            w_regroup(g)
+            if g > 0:
+                w_quant(g - 1)
+        w_quant(3)
+
+        state = {"front": 0, "quant": 0}
+
+        def front(n):
+            for i in range(n):
+                if state["front"] < NP:
+                    x_front(state["front"])
+                    state["front"] += 1
+                    if state["front"] - 1 > state["quant"]:
+                        x_quant(state["quant"])
+                        state["quant"] += 1
+
+        def flush_quant():
+            while state["quant"] < state["front"]:
+                x_quant(state["quant"])
+                state["quant"] += 1
+
+        front(FRONT_FIRST)
+        h_half(0)
+        flush_quant()
+        for k in range(MX_AHEAD):
+            mx_pair(k)
+        for s in range(NP + 3):
+            if s < NP:
+                gates(2 * s)
+                gates(2 * s + 1)
+            if 0 <= s - 1 < NP:
+                cell(s - 1)
+            if 0 <= s - 2 < G_PAIRS:
+                cell_tanh(s - 2)
+            if G_PAIRS <= s - 1 < NP:
+                cell_tanh(s - 1)
+            if 0 <= s - 3 < G_PAIRS:
+                hidden(s - 3)
+            if G_PAIRS <= s - 2 < NP:
+                hidden(s - 2)
+            if state["front"] < NP:
+                front(FRONT_STEP)
+                if state["front"] >= NP:
+                    flush_quant()
+            if s == H1_AT:
+                h_half(1)
+            if s + MX_AHEAD < NP:
+                mx_pair(s + MX_AHEAD)

@@ -20,13 +20,14 @@ D = 512
 U = 128
 G4 = 4 * U
 
-MX_AHEAD = 2
-FRONT_FIRST = 3
-FRONT_STEP = 2
-H1_AT = 2
-G_PAIRS = 5
-S_COPIES = 5
-V_ADD = (1,)
+DIRECT = ()
+X_ON_SCALAR = (0, 1)
+M1_ON_SCALAR = (0, 1, 2, 3, 4, 5, 6, 7)
+POOL_IB = (0, 1, 2, 3, 4)
+POOL_FA = (0, 1, 2, 3, 4, 5)
+POOL_H = ()
+POOL_C = ()
+TAIL = 7
 
 
 def tile_lstm_kernel(tc, pre_layer, x, W_i, W_f, W_o, W_c, U_i, U_f, U_o, U_c, out):
@@ -44,29 +45,40 @@ def tile_lstm_kernel(tc, pre_layer, x, W_i, W_f, W_o, W_c, U_i, U_f, U_o, U_c, o
         x_sb = [keep.tile([P, 2 * D], BF16, name="x%d" % k) for k in range(NP)]
         w_raw = [keep.tile([P, 4 * U], BF16, name="w_raw%d" % g) for g in range(4)]
         u_sb = keep.tile([P, G4], BF16, name="u_sb")
-        ph_sb = [keep.tile([P, 8, U], BF16, name="ph%d" % i) for i in range(2)]
-        pc_sb = keep.tile([P, NT, U], BF16, name="pc_sb")
+        ph_sb = [keep.tile([P, 4, U], BF16, name="ph%d" % i) for i in range(4)]
+        pc_sb = [keep.tile([P, 8, U], BF16, name="pc%d" % i) for i in range(2)]
 
         def load_x(k):
             nc.sync.dma_start(
                 out=x_sb[k][:].rearrange("p (t k) -> p t k", t=2), in_=xv[:, 2 * k : 2 * k + 2, :]
             )
 
+        def load_h(i, queue):
+            queue.dma_start(out=ph_sb[i][:], in_=prev[0, :, 4 * i : 4 * i + 4, :])
+
+        def load_c(i):
+            nc.sync.dma_start(out=pc_sb[i][:], in_=prev[1, :, 8 * i : 8 * i + 8, :])
+
         load_x(0)
-        nc.scalar.dma_start(out=ph_sb[0][:], in_=prev[0, :, 0:8, :])
-        for g, w in enumerate((W_i, W_f, W_o, W_c)):
-            nc.sync.dma_start(
-                out=w_raw[g][:],
-                in_=w.rearrange("(q e) c -> q (e c)", e=4),
-            )
-        for g, uw in enumerate((U_i, U_f, U_o, U_c)):
-            nc.scalar.dma_start(out=u_sb[:, g * U : (g + 1) * U], in_=uw)
-        for k in (1, 2, 3, 4, 5):
-            load_x(k)
-        nc.sync.dma_start(out=pc_sb[:], in_=prev[1])
+        load_h(0, nc.scalar)
+        w_all = (W_i, W_f, W_o, W_c)
+        u_all = (U_i, U_f, U_o, U_c)
+        for g in range(4):
+            nc.sync.dma_start(out=w_raw[g][:], in_=w_all[g].rearrange("(q e) c -> q (e c)", e=4))
+        load_x(1)
+        for g in range(4):
+            nc.sync.dma_start(out=u_sb[:, g * U : (g + 1) * U], in_=u_all[g])
+        load_x(2)
+        load_h(1, nc.sync)
+        load_x(3)
+        load_c(0)
+        load_x(4)
+        load_h(2, nc.sync)
+        load_x(5)
         load_x(6)
+        load_c(1)
+        load_h(3, nc.sync)
         load_x(7)
-        nc.sync.dma_start(out=ph_sb[1][:], in_=prev[0, :, 8:16, :])
 
         ident_f = keep.tile([P, P], F32, name="ident_f")
         make_identity(nc, ident_f[:])
@@ -82,13 +94,15 @@ def tile_lstm_kernel(tc, pre_layer, x, W_i, W_f, W_o, W_c, U_i, U_f, U_o, U_c, o
         ws = keep.tile([P, G4], U8, name="ws", align_bytes=64)
         xq = keep.tile([P, NT * P], U32, name="xq", align_bytes=64)
         xs = keep.tile([P, NT * P], U8, name="xs", align_bytes=64)
-        hT_sb = [keep.tile([P, 8 * P], BF16, name="hT%d" % i) for i in range(2)]
+        hT_sb = [keep.tile([P, 4 * P], BF16, name="hT%d" % i) for i in range(4)]
 
-        def w_regroup(g):
-            nc.vector.tensor_copy(
-                out=wg[:, g * 4 * U : (g + 1) * 4 * U].rearrange("p (c t) -> p c t", t=4),
-                in_=w_raw[g][:].rearrange("p (t c) -> p c t", t=4),
-            )
+        def w_regroup(g, on_pool):
+            dst = wg[:, g * 4 * U : (g + 1) * 4 * U].rearrange("p (c t) -> p c t", t=4)
+            src = w_raw[g][:].rearrange("p (t c) -> p c t", t=4)
+            if on_pool:
+                nc.gpsimd.tensor_scalar(out=dst, in0=src, scalar1=1.0, scalar2=0.0, op0=ALU.mult, op1=ALU.add)
+            else:
+                nc.vector.tensor_copy(out=dst, in_=src)
 
         def w_quant(g):
             nc.vector.quantize_mx(
@@ -97,195 +111,229 @@ def tile_lstm_kernel(tc, pre_layer, x, W_i, W_f, W_o, W_c, U_i, U_f, U_o, U_c, o
                 in_=wg[:, g * 4 * U : (g + 1) * 4 * U],
             )
 
-        xg_of = {}
+        xt_of, xg_of, ht_of, mx_of, ms_of, ps_of, zt_of, a_of, c_of = {}, {}, {}, {}, {}, {}, {}, {}, {}
 
-        def x_front(k):
-            xt = psum.tile([P, 2, 2, P], F32, name="xt", tag="tz", bufs=4)
+        def x_transpose(k):
+            xt = psum.tile([P, 2, 2, P], F32, name="xt", tag="tz", bufs=6)
             xw = x_sb[k][:].bitcast(F32)
             for j in range(2):
                 for u in range(2):
                     words = xw[:, j * (D // 2) + u : (j + 1) * (D // 2) : 2]
                     nc.tensor.transpose(xt[:, j, u, :], words, ident_f[:])
+            xt_of[k] = xt
+
+        def x_copy(k):
             xg = work.tile([P, 2 * D], BF16, name="xg", tag="xg", align_bytes=64)
             dst = xg[:].bitcast(F32).rearrange("p (j r u) -> p j r u", j=2, r=P, u=2)
-            src = xt[:].rearrange("p j u r -> p j r u")
-            if k % 2 == 1:
-                nc.vector.tensor_copy(out=dst, in_=src)
-            else:
+            src = xt_of[k][:].rearrange("p j u r -> p j r u")
+            if k in X_ON_SCALAR:
                 nc.scalar.copy(out=dst, in_=src)
+            else:
+                nc.vector.tensor_copy(out=dst, in_=src)
             xg_of[k] = xg
 
         def x_quant(k):
             cols = slice(2 * k * P, (2 * k + 2) * P)
             nc.vector.quantize_mx(out=xq[:, cols].bitcast(FP8X4), scales=xs[:, cols], in_=xg_of[k][:])
 
-        def h_half(i):
-            ht = psum.tile([P, 8, P], BF16, name="ht", tag="tz", bufs=4)
-            for j in range(8):
+        def h_transpose(i):
+            ht = psum.tile([P, 4, P], BF16, name="ht", tag="tz", bufs=6)
+            for j in range(4):
                 nc.tensor.transpose(ht[:, j, :], ph_sb[i][:, j, :], ident_b[:])
-            nc.scalar.copy(out=hT_sb[i][:], in_=ht[:].rearrange("p j r -> p (j r)"))
+            ht_of[i] = ht
 
-        mt_of = {}
+        def h_copy(i):
+            nc.scalar.copy(out=hT_sb[i][:], in_=ht_of[i][:].rearrange("p j r -> p (j r)"))
 
-        z_of = {}
+        def hT(t):
+            return hT_sb[t // 4][:, (t % 4) * P : (t % 4 + 1) * P]
 
-        def mx_pair_plain_sum(k):
-            mxs = []
+        def plain(k):
+            banks = []
             for j in range(2):
-                t = 2 * k + j
-                cols = slice(t * P, (t + 1) * P)
-                mx = psum.tile([P, G4], F32, name="mx", tag="mt", bufs=4)
-                nc.tensor.matmul_mx(
-                    out=mx[:],
-                    lhsT=xq[:, cols].bitcast(FP8X4),
-                    lhsT_scale=xs[:, cols],
-                    rhs=wq[:].bitcast(FP8X4),
-                    rhs_scale=ws[:],
-                    start=True,
-                    stop=True,
-                )
-                mxs.append(mx)
-            pps = []
-            for j in range(2):
-                t = 2 * k + j
-                pp = psum.tile([P, G4], F32, name="pp", tag="tz", bufs=4)
-                nc.tensor.matmul(
-                    out=pp[:], lhsT=hT_sb[t // 8][:, (t % 8) * P : (t % 8 + 1) * P], rhs=u_sb[:], start=True, stop=True
-                )
-                pps.append(pp)
+                z = psum.tile([P, G4], F32, name="z", tag="tz", bufs=6)
+                nc.tensor.matmul(out=z[:], lhsT=hT(2 * k + j), rhs=u_sb[:], start=True, stop=(k in DIRECT))
+                banks.append(z)
+            zt_of[k] = banks
+
+        def plain_copy(k):
             z_sb = work.tile([P, 2, G4], F32, name="z_sb", tag="z_sb")
             for j in range(2):
-                nc.scalar.copy(out=z_sb[:, j, :], in_=pps[j][:])
-            for j in range(2):
-                nc.vector.tensor_tensor(out=z_sb[:, j, :], in0=mxs[j][:], in1=z_sb[:, j, :], op=ALU.add)
-            z_of[k] = z_sb
+                nc.scalar.copy(out=z_sb[:, j, :], in_=zt_of[k][j][:])
+            ps_of[k] = z_sb
 
-        def mx_pair(k):
-            if k in V_ADD:
-                mx_pair_plain_sum(k)
-                return
-            cols = slice(2 * k * P, (2 * k + 2) * P)
-            for b in range(2):
-                mt = psum.tile([P, 2, 2 * P], F32, name="mt", tag="mt", bufs=4)
-                for gg in range(2):
-                    g = 2 * b + gg
+        def mx(k):
+            banks = []
+            if k in DIRECT:
+                for j in range(2):
+                    cols = slice((2 * k + j) * P, (2 * k + j + 1) * P)
+                    m = psum.tile([P, G4], F32, name="m", tag="mt", bufs=2)
                     nc.tensor.matmul_mx(
-                        out=mt[:, gg, :],
-                        lhsT=wq[:, g * U : (g + 1) * U].bitcast(FP8X4),
-                        lhsT_scale=ws[:, g * U : (g + 1) * U],
-                        rhs=xq[:, cols].bitcast(FP8X4),
-                        rhs_scale=xs[:, cols],
+                        out=m[:],
+                        lhsT=xq[:, cols].bitcast(FP8X4),
+                        lhsT_scale=xs[:, cols],
+                        rhs=wq[:].bitcast(FP8X4),
+                        rhs_scale=ws[:],
                         start=True,
                         stop=True,
                     )
-                mt_sb = work.tile([P, 2, 2 * P], F32, name="mt_sb%d" % b, tag="mt_sb%d" % b)
-                if b == 0 or k >= S_COPIES:
-                    nc.vector.tensor_copy(out=mt_sb[:], in_=mt[:])
-                else:
-                    nc.scalar.copy(out=mt_sb[:], in_=mt[:])
-                mt_of[(k, b)] = mt_sb
+                    banks.append(m)
+            else:
+                cols = slice(2 * k * P, (2 * k + 2) * P)
+                for b in range(2):
+                    mt = psum.tile([P, 2, 2 * P], F32, name="mt", tag="mt", bufs=2)
+                    for gg in range(2):
+                        g = 2 * b + gg
+                        nc.tensor.matmul_mx(
+                            out=mt[:, gg, :],
+                            lhsT=wq[:, g * U : (g + 1) * U].bitcast(FP8X4),
+                            lhsT_scale=ws[:, g * U : (g + 1) * U],
+                            rhs=xq[:, cols].bitcast(FP8X4),
+                            rhs_scale=xs[:, cols],
+                            start=True,
+                            stop=True,
+                        )
+                    banks.append(mt)
+            mx_of[k] = banks
 
-        a_of = {}
-
-        def gates(t):
-            k, j = t // 2, t % 2
-            if j == 0:
-                a_new = work.tile([P, 2, G4], F32, name="a", tag="a")
-                a_of[k] = a_new
-            a = a_of[k]
-            if k in V_ADD:
-                if j == 0:
-                    z_sb = z_of[k]
-                    nc.scalar.activation(out=a[:, :, 0 : 3 * U], in_=z_sb[:, :, 0 : 3 * U], func=ACT.Sigmoid)
-                    nc.scalar.activation(out=a[:, :, 3 * U : G4], in_=z_sb[:, :, 3 * U : G4], func=ACT.Tanh)
+        def mx_out(k):
+            if k in DIRECT:
+                z_sb = ps_of[k]
+                for j in range(2):
+                    nc.vector.tensor_tensor(out=z_sb[:, j, :], in0=mx_of[k][j][:], in1=z_sb[:, j, :], op=ALU.add)
                 return
-            zt = psum.tile([P, G4], F32, name="zt", tag="tz", bufs=4)
-            nc.tensor.matmul(
-                out=zt[:], lhsT=hT_sb[t // 8][:, (t % 8) * P : (t % 8 + 1) * P], rhs=u_sb[:], start=True, stop=False
-            )
-            for g in range(4):
-                nc.tensor.matmul(
-                    out=zt[:, g * U : (g + 1) * U],
-                    lhsT=mt_of[(k, g // 2)][:, g % 2, j * P : (j + 1) * P],
-                    rhs=ident_f[:],
-                    is_transpose=True,
-                    start=False,
-                    stop=(g == 3),
-                )
-            nc.scalar.activation(out=a[:, j, 0 : 3 * U], in_=zt[:, 0 : 3 * U], func=ACT.Sigmoid)
-            nc.scalar.activation(out=a[:, j, 3 * U : G4], in_=zt[:, 3 * U : G4], func=ACT.Tanh)
+            tiles = []
+            for b in range(2):
+                mt_sb = work.tile([P, 2, 2 * P], F32, name="mt_sb%d" % b, tag="mt_sb%d" % b)
+                if b == 1 and k in M1_ON_SCALAR:
+                    nc.scalar.copy(out=mt_sb[:], in_=mx_of[k][b][:])
+                else:
+                    nc.vector.tensor_copy(out=mt_sb[:], in_=mx_of[k][b][:])
+                tiles.append(mt_sb)
+            ms_of[k] = tiles
 
-        tc_of = {}
-        c_of = {}
+        def add_back(k):
+            if k in DIRECT:
+                return
+            for j in range(2):
+                for g in range(4):
+                    nc.tensor.matmul(
+                        out=zt_of[k][j][:, g * U : (g + 1) * U],
+                        lhsT=ms_of[k][g // 2][:, g % 2, j * P : (j + 1) * P],
+                        rhs=ident_f[:],
+                        is_transpose=True,
+                        start=False,
+                        stop=(g == 3),
+                    )
 
-        def cell(k):
-            eng = nc.gpsimd if k < G_PAIRS else nc.vector
-            a = a_of[k]
+        def gates(k):
+            a = work.tile([P, 2, G4], F32, name="a", tag="a")
+            a_of[k] = a
+            if k in DIRECT:
+                z_sb = ps_of[k]
+                nc.scalar.activation(out=a[:, :, 0 : 3 * U], in_=z_sb[:, :, 0 : 3 * U], func=ACT.Sigmoid)
+                nc.scalar.activation(out=a[:, :, 3 * U : G4], in_=z_sb[:, :, 3 * U : G4], func=ACT.Tanh)
+                return
+            for j in range(2):
+                z = zt_of[k][j]
+                nc.scalar.activation(out=a[:, j, 0 : 3 * U], in_=z[:, 0 : 3 * U], func=ACT.Sigmoid)
+                nc.scalar.activation(out=a[:, j, 3 * U : G4], in_=z[:, 3 * U : G4], func=ACT.Tanh)
+
+        def new_cell(k):
             fa = work.tile([P, 2, U], F32, name="fa", tag="fa")
-            eng.tensor_tensor(out=fa[:], in0=a[:, :, U : 2 * U], in1=pc_sb[:, 2 * k : 2 * k + 2, :], op=ALU.mult)
             ib = work.tile([P, 2, U], F32, name="ib", tag="ib")
-            eng.tensor_tensor(out=ib[:], in0=a[:, :, 0:U], in1=a[:, :, 3 * U : G4], op=ALU.mult)
             c_sb = work.tile([P, 2, U], F32, name="c_sb", tag="c_sb")
-            eng.tensor_tensor(out=c_sb[:], in0=fa[:], in1=ib[:], op=ALU.add)
-            nc.sync.dma_start(out=outv[1, :, 2 * k : 2 * k + 2, :], in_=c_sb[:])
-            c_of[k] = c_sb
-
-        def cell_tanh(k):
             tc_sb = work.tile([P, 2, U], F32, name="tc_sb", tag="tc_sb")
-            nc.scalar.activation(out=tc_sb[:], in_=c_of[k][:], func=ACT.Tanh)
-            tc_of[k] = tc_sb
-
-        def hidden(k):
             h_sb = work.tile([P, 2, U], F32, name="h_sb", tag="h_sb")
-            nc.vector.tensor_tensor(out=h_sb[:], in0=a_of[k][:, :, 2 * U : 3 * U], in1=tc_of[k][:], op=ALU.mult)
-            nc.sync.dma_start(out=outv[0, :, 2 * k : 2 * k + 2, :], in_=h_sb[:])
+            c_of[k] = (fa, ib, c_sb, tc_sb, h_sb)
 
-        for g in range(4):
-            w_regroup(g)
-            if g > 0:
-                w_quant(g - 1)
-        w_quant(3)
+        ALL = slice(0, 2)
 
-        state = {"front": 0, "quant": 0}
+        def cell_mul(k, js=ALL):
+            fa, ib = c_of[k][0], c_of[k][1]
+            a = a_of[k]
+            t0 = (2 * k) % 8
+            pc = pc_sb[k // 4][:, t0 + js.start : t0 + js.stop, :]
+            eng = nc.gpsimd if k in POOL_FA else nc.vector
+            eng.tensor_tensor(out=fa[:, js], in0=a[:, js, U : 2 * U], in1=pc, op=ALU.mult)
+            eng = nc.gpsimd if k in POOL_IB else nc.vector
+            eng.tensor_tensor(out=ib[:, js], in0=a[:, js, 0:U], in1=a[:, js, 3 * U : G4], op=ALU.mult)
 
-        def front(n):
-            for i in range(n):
-                if state["front"] < NP:
-                    x_front(state["front"])
-                    state["front"] += 1
-                    if state["front"] - 1 > state["quant"]:
-                        x_quant(state["quant"])
-                        state["quant"] += 1
+        def cell_add(k, js=ALL):
+            fa, ib, c_sb = c_of[k][0], c_of[k][1], c_of[k][2]
+            eng = nc.gpsimd if k in POOL_C else nc.vector
+            eng.tensor_tensor(out=c_sb[:, js], in0=fa[:, js], in1=ib[:, js], op=ALU.add)
+            nc.sync.dma_start(out=outv[1, :, 2 * k + js.start : 2 * k + js.stop, :], in_=c_sb[:, js])
 
-        def flush_quant():
-            while state["quant"] < state["front"]:
-                x_quant(state["quant"])
-                state["quant"] += 1
+        def cell_tanh(k, js=ALL):
+            nc.scalar.activation(out=c_of[k][3][:, js], in_=c_of[k][2][:, js], func=ACT.Tanh)
 
-        front(FRONT_FIRST)
-        h_half(0)
-        flush_quant()
-        for k in range(MX_AHEAD):
-            mx_pair(k)
-        for s in range(NP + 3):
-            if s < NP:
-                gates(2 * s)
-                gates(2 * s + 1)
-            if 0 <= s - 1 < NP:
-                cell(s - 1)
-            if 0 <= s - 2 < G_PAIRS:
+        def hidden(k, js=ALL):
+            tc_sb, h_sb = c_of[k][3], c_of[k][4]
+            eng = nc.gpsimd if k in POOL_H else nc.vector
+            eng.tensor_tensor(out=h_sb[:, js], in0=a_of[k][:, js, 2 * U : 3 * U], in1=tc_sb[:, js], op=ALU.mult)
+            nc.sync.dma_start(out=outv[0, :, 2 * k + js.start : 2 * k + js.stop, :], in_=h_sb[:, js])
+
+        x_transpose(0)
+        h_transpose(0)
+        for s in range(-2, NP + 2):
+            if s == -2:
+                x_copy(0)
+                h_copy(0)
+                w_regroup(0, False)
+                w_regroup(1, False)
+                w_quant(0)
+                w_regroup(2, False)
+                w_quant(1)
+                x_quant(0)
+                w_regroup(3, False)
+                w_quant(2)
+                x_transpose(1)
+                w_quant(3)
+                continue
+            if s + 2 < NP:
+                x_copy(s + 2)
+            if s + 1 in DIRECT:
+                plain(s + 1)
+            if s + 1 < NP:
+                mx(s + 1)
+            if 0 <= s - 2 < TAIL:
                 cell_tanh(s - 2)
-            if G_PAIRS <= s - 1 < NP:
-                cell_tanh(s - 1)
-            if 0 <= s - 3 < G_PAIRS:
-                hidden(s - 3)
-            if G_PAIRS <= s - 2 < NP:
+            if s + 1 < NP and s + 1 not in DIRECT:
+                mx_out(s + 1)
+            if s + 1 in DIRECT:
+                plain_copy(s + 1)
+            if 0 <= s < NP:
+                if s not in DIRECT:
+                    plain(s)
+                    add_back(s)
+                gates(s)
+                new_cell(s)
+            if s + 2 < NP:
+                x_quant(s + 2)
+            if 0 <= s - 2 < TAIL:
                 hidden(s - 2)
-            if state["front"] < NP:
-                front(FRONT_STEP)
-                if state["front"] >= NP:
-                    flush_quant()
-            if s == H1_AT:
-                h_half(1)
-            if s + MX_AHEAD < NP:
-                mx_pair(s + MX_AHEAD)
+            if 0 <= s - 1 < TAIL:
+                cell_mul(s - 1)
+                cell_add(s - 1)
+            if s + 1 in DIRECT:
+                mx_out(s + 1)
+            if s + 3 < NP:
+                x_transpose(s + 3)
+            if s in (-1, 1, 3):
+                h_transpose((s + 1) // 2 + 1)
+                h_copy((s + 1) // 2 + 1)
+            if TAIL <= s < NP:
+                if s == NP - 1:
+                    for j in range(2):
+                        js = slice(j, j + 1)
+                        cell_mul(s, js)
+                        cell_add(s, js)
+                        cell_tanh(s, js)
+                    for j in range(2):
+                        hidden(s, slice(j, j + 1))
+                else:
+                    cell_mul(s)
+                    cell_add(s)
+                    cell_tanh(s)
+                    hidden(s)

@@ -27,7 +27,7 @@ POOL_IB = (0, 1, 2, 3, 4)
 POOL_FA = (0, 1, 2, 3, 4, 5)
 POOL_H = ()
 POOL_C = ()
-TAIL = 7
+TAIL = 6
 
 
 def tile_lstm_kernel(tc, pre_layer, x, W_i, W_f, W_o, W_c, U_i, U_f, U_o, U_c, out):
@@ -96,11 +96,11 @@ def tile_lstm_kernel(tc, pre_layer, x, W_i, W_f, W_o, W_c, U_i, U_f, U_o, U_c, o
         xs = keep.tile([P, NT * P], U8, name="xs", align_bytes=64)
         hT_sb = [keep.tile([P, 4 * P], BF16, name="hT%d" % i) for i in range(4)]
 
-        def w_regroup(g, on_pool):
+        def w_regroup(g, on_scalar):
             dst = wg[:, g * 4 * U : (g + 1) * 4 * U].rearrange("p (c t) -> p c t", t=4)
             src = w_raw[g][:].rearrange("p (t c) -> p c t", t=4)
-            if on_pool:
-                nc.gpsimd.tensor_scalar(out=dst, in0=src, scalar1=1.0, scalar2=0.0, op0=ALU.mult, op1=ALU.add)
+            if on_scalar:
+                nc.scalar.copy(out=dst, in_=src)
             else:
                 nc.vector.tensor_copy(out=dst, in_=src)
 
@@ -236,6 +236,11 @@ def tile_lstm_kernel(tc, pre_layer, x, W_i, W_f, W_o, W_c, U_i, U_f, U_o, U_c, o
                 return
             for j in range(2):
                 z = zt_of[k][j]
+                if k == NP - 1:
+                    nc.scalar.activation(out=a[:, j, 0 : 2 * U], in_=z[:, 0 : 2 * U], func=ACT.Sigmoid)
+                    nc.scalar.activation(out=a[:, j, 3 * U : G4], in_=z[:, 3 * U : G4], func=ACT.Tanh)
+                    nc.scalar.activation(out=a[:, j, 2 * U : 3 * U], in_=z[:, 2 * U : 3 * U], func=ACT.Sigmoid)
+                    continue
                 nc.scalar.activation(out=a[:, j, 0 : 3 * U], in_=z[:, 0 : 3 * U], func=ACT.Sigmoid)
                 nc.scalar.activation(out=a[:, j, 3 * U : G4], in_=z[:, 3 * U : G4], func=ACT.Tanh)
 
@@ -276,64 +281,55 @@ def tile_lstm_kernel(tc, pre_layer, x, W_i, W_f, W_o, W_c, U_i, U_f, U_o, U_c, o
 
         x_transpose(0)
         h_transpose(0)
-        for s in range(-2, NP + 2):
-            if s == -2:
-                x_copy(0)
-                h_copy(0)
-                w_regroup(0, False)
-                w_regroup(1, False)
-                w_quant(0)
-                w_regroup(2, False)
-                w_quant(1)
-                x_quant(0)
-                w_regroup(3, False)
-                w_quant(2)
-                x_transpose(1)
-                w_quant(3)
-                continue
+        x_copy(0)
+        h_copy(0)
+        w_regroup(0, False)
+        w_regroup(1, False)
+        w_quant(0)
+        w_regroup(2, False)
+        w_quant(1)
+        x_quant(0)
+        w_regroup(3, False)
+        w_quant(2)
+        x_transpose(1)
+        w_quant(3)
+        for s in range(-1, NP):
             if s + 2 < NP:
                 x_copy(s + 2)
-            if s + 1 in DIRECT:
-                plain(s + 1)
             if s + 1 < NP:
                 mx(s + 1)
-            if 0 <= s - 2 < TAIL:
+            if 0 <= s - 2:
                 cell_tanh(s - 2)
-            if s + 1 < NP and s + 1 not in DIRECT:
+            if s + 1 < NP:
                 mx_out(s + 1)
-            if s + 1 in DIRECT:
-                plain_copy(s + 1)
-            if 0 <= s < NP:
-                if s not in DIRECT:
-                    plain(s)
-                    add_back(s)
+            if 0 <= s:
+                plain(s)
+                add_back(s)
                 gates(s)
                 new_cell(s)
             if s + 2 < NP:
                 x_quant(s + 2)
-            if 0 <= s - 2 < TAIL:
+            if s == NP - 1:
+                break
+            if 0 <= s - 2:
                 hidden(s - 2)
-            if 0 <= s - 1 < TAIL:
+            if 0 <= s - 1:
                 cell_mul(s - 1)
                 cell_add(s - 1)
-            if s + 1 in DIRECT:
-                mx_out(s + 1)
             if s + 3 < NP:
                 x_transpose(s + 3)
             if s in (-1, 1, 3):
                 h_transpose((s + 1) // 2 + 1)
                 h_copy((s + 1) // 2 + 1)
-            if TAIL <= s < NP:
-                if s == NP - 1:
-                    for j in range(2):
-                        js = slice(j, j + 1)
-                        cell_mul(s, js)
-                        cell_add(s, js)
-                        cell_tanh(s, js)
-                    for j in range(2):
-                        hidden(s, slice(j, j + 1))
-                else:
-                    cell_mul(s)
-                    cell_add(s)
-                    cell_tanh(s)
-                    hidden(s)
+        cell_mul(NP - 2)
+        cell_add(NP - 2)
+        hidden(NP - 3)
+        cell_tanh(NP - 2)
+        for j in range(2):
+            js = slice(j, j + 1)
+            cell_mul(NP - 1, js)
+            cell_add(NP - 1, js)
+            cell_tanh(NP - 1, js)
+        hidden(NP - 2)
+        for j in range(2):
+            hidden(NP - 1, slice(j, j + 1))

@@ -148,18 +148,15 @@ def tile_lstm_kernel(tc, pre_layer, x, W_i, W_f, W_o, W_c, U_i, U_f, U_o, U_c, o
         def hT(t):
             return hT_sb[t // 4][:, (t % 4) * P : (t % 4 + 1) * P]
 
-        def plain(k):
-            banks = []
-            for j in range(2):
-                z = psum.tile([P, G4], F32, name="z", tag="tz", bufs=6)
-                nc.tensor.matmul(out=z[:], lhsT=hT(2 * k + j), rhs=u_sb[:], start=True, stop=(k in DIRECT))
-                banks.append(z)
-            zt_of[k] = banks
+        def plain(k, j):
+            z = psum.tile([P, G4], F32, name="z", tag="tz", bufs=6)
+            nc.tensor.matmul(out=z[:], lhsT=hT(2 * k + j), rhs=u_sb[:], start=True, stop=False)
+            zt_of[(k, j)] = z
 
         def plain_copy(k):
             z_sb = work.tile([P, 2, G4], F32, name="z_sb", tag="z_sb")
             for j in range(2):
-                nc.scalar.copy(out=z_sb[:, j, :], in_=zt_of[k][j][:])
+                nc.scalar.copy(out=z_sb[:, j, :], in_=zt_of[(k, j)][:])
             ps_of[k] = z_sb
 
         def mx(k):
@@ -218,7 +215,7 @@ def tile_lstm_kernel(tc, pre_layer, x, W_i, W_f, W_o, W_c, U_i, U_f, U_o, U_c, o
             for j in range(2):
                 for g in range(4):
                     nc.tensor.matmul(
-                        out=zt_of[k][j][:, g * U : (g + 1) * U],
+                        out=zt_of[(k, j)][:, g * U : (g + 1) * U],
                         lhsT=ms_of[k][g // 2][:, g % 2, j * P : (j + 1) * P],
                         rhs=ident_f[:],
                         is_transpose=True,
@@ -235,7 +232,7 @@ def tile_lstm_kernel(tc, pre_layer, x, W_i, W_f, W_o, W_c, U_i, U_f, U_o, U_c, o
                 nc.scalar.activation(out=a[:, :, 3 * U : G4], in_=z_sb[:, :, 3 * U : G4], func=ACT.Tanh)
                 return
             for j in range(2):
-                z = zt_of[k][j]
+                z = zt_of[(k, j)]
                 if k == NP - 1:
                     nc.scalar.activation(out=a[:, j, 0 : 2 * U], in_=z[:, 0 : 2 * U], func=ACT.Sigmoid)
                     nc.scalar.activation(out=a[:, j, 3 * U : G4], in_=z[:, 3 * U : G4], func=ACT.Tanh)
@@ -296,15 +293,18 @@ def tile_lstm_kernel(tc, pre_layer, x, W_i, W_f, W_o, W_c, U_i, U_f, U_o, U_c, o
         for s in range(-1, NP):
             if s + 2 < NP:
                 x_copy(s + 2)
+            if 0 <= s:
+                plain(s, 0)
             if s + 1 < NP:
                 mx(s + 1)
-            if 0 <= s - 2:
+            if 0 <= s - 2 and s < NP - 1:
                 cell_tanh(s - 2)
-            if s + 1 < NP:
+            if s + 1 < NP and s + 1 not in DIRECT:
                 mx_out(s + 1)
             if 0 <= s:
-                plain(s)
-                add_back(s)
+                if s not in DIRECT:
+                    plain(s, 1)
+                    add_back(s)
                 gates(s)
                 new_cell(s)
             if s + 2 < NP:
@@ -316,20 +316,25 @@ def tile_lstm_kernel(tc, pre_layer, x, W_i, W_f, W_o, W_c, U_i, U_f, U_o, U_c, o
             if 0 <= s - 1:
                 cell_mul(s - 1)
                 cell_add(s - 1)
+            if s + 1 in DIRECT:
+                mx_out(s + 1)
             if s + 3 < NP:
                 x_transpose(s + 3)
             if s in (-1, 1, 3):
                 h_transpose((s + 1) // 2 + 1)
                 h_copy((s + 1) // 2 + 1)
-        cell_mul(NP - 2)
+        halves = (slice(0, 1), slice(1, 2))
+        cell_tanh(NP - 3)
+        for js in halves:
+            cell_mul(NP - 2, js)
         cell_add(NP - 2)
-        hidden(NP - 3)
         cell_tanh(NP - 2)
-        for j in range(2):
-            js = slice(j, j + 1)
+        for js in halves:
             cell_mul(NP - 1, js)
+        hidden(NP - 3)
+        for js in halves:
             cell_add(NP - 1, js)
             cell_tanh(NP - 1, js)
         hidden(NP - 2)
-        for j in range(2):
-            hidden(NP - 1, slice(j, j + 1))
+        for js in halves:
+            hidden(NP - 1, js)

@@ -65,7 +65,8 @@ def tile_lstm_kernel(tc, pre_layer, x, W_i, W_f, W_o, W_c, U_i, U_f, U_o, U_c, o
         u_all = (U_i, U_f, U_o, U_c)
         for g in range(4):
             nc.sync.dma_start(out=w_raw[g][:], in_=w_all[g].rearrange("(q e) c -> q (e c)", e=4))
-        load_x(1)
+            if g == 1:
+                load_x(1)
         for g in range(4):
             nc.sync.dma_start(out=u_sb[:, g * U : (g + 1) * U], in_=u_all[g])
         load_x(2)
@@ -331,10 +332,10 @@ def tile_lstm_kernel(tc, pre_layer, x, W_i, W_f, W_o, W_c, U_i, U_f, U_o, U_c, o
         cell_tanh(NP - 2)
         for js in halves:
             cell_mul(NP - 1, js)
-        hidden(NP - 3)
         for js in halves:
             cell_add(NP - 1, js)
             cell_tanh(NP - 1, js)
+        hidden(NP - 3)
         hidden(NP - 2)
         for js in halves:
             hidden(NP - 1, js)

from contextlib import ExitStack

import concourse.mybir as mybir
from concourse.masks import make_identity

FLOPS = 2 * 2048 * 512 * 512 + 2 * 2048 * 128 * 512

F32 = mybir.dt.float32
BF16 = mybir.dt.bfloat16
U32 = mybir.dt.uint32
U8 = mybir.dt.uint8
FP8X4 = mybir.dt.float8_e4m3fn_x4
ACT = mybir.ActivationFunctionType
ALU = mybir.AluOpType

P = 128
NT = 16
NP = NT // 2
D = 512
U = 128
G4 = 4 * U

DIRECT = ()
X_ON_SCALAR = (0, 1)
M1_ON_SCALAR = (0, 1, 2, 3, 4, 5, 6, 7)
POOL_IB = (0, 1, 2, 3, 4)
POOL_FA = (0, 1, 2, 3, 4, 5)
POOL_H = ()
POOL_C = ()
TAIL = 6


def tile_lstm_kernel(tc, pre_layer, x, W_i, W_f, W_o, W_c, U_i, U_f, U_o, U_c, out):
    nc = tc.nc
    with ExitStack() as ctx:
        keep = ctx.enter_context(tc.tile_pool(name="keep", bufs=1))
        work = ctx.enter_context(tc.tile_pool(name="work", bufs=5))
        psum = ctx.enter_context(tc.psum_pool(name="psum", bufs=2))
        ctx.enter_context(tc.manual_schedule())

        xv = x.rearrange("(p t) k -> p t k", t=NT)
        prev = pre_layer.rearrange("s (p t) u -> s p t u", t=NT)
        outv = out.rearrange("s (p t) u -> s p t u", t=NT)

        x_sb = [keep.tile([P, 2 * D], BF16, name="x%d" % k) for k in range(NP)]
        w_raw = [keep.tile([P, 4 * U], BF16, name="w_raw%d" % g) for g in range(4)]
        u_sb = keep.tile([P, G4], BF16, name="u_sb")
        ph_sb = [keep.tile([P, 4, U], BF16, name="ph%d" % i) for i in range(4)]
        pc_sb = [keep.tile([P, 8, U], BF16, name="pc%d" % i) for i in range(2)]

        def load_x(k):
            nc.sync.dma_start(
                out=x_sb[k][:].rearrange("p (t k) -> p t k", t=2), in_=xv[:, 2 * k : 2 * k + 2, :]
            )

        def load_h(i, queue):
            queue.dma_start(out=ph_sb[i][:], in_=prev[0, :, 4 * i : 4 * i + 4, :])

        def load_c(i):
            nc.sync.dma_start(out=pc_sb[i][:], in_=prev[1, :, 8 * i : 8 * i + 8, :])

        load_x(0)
        load_h(0, nc.scalar)
        w_all = (W_i, W_f, W_o, W_c)
        u_all = (U_i, U_f, U_o, U_c)
        for g in range(4):
            nc.sync.dma_start(out=w_raw[g][:], in_=w_all[g].rearrange("(q e) c -> q (e c)", e=4))
            if g == 1:
                load_x(1)
        for g in range(4):
            nc.sync.dma_start(out=u_sb[:, g * U : (g + 1) * U], in_=u_all[g])
        load_x(2)
        load_h(1, nc.sync)
        load_x(3)
        load_c(0)
        load_x(4)
        load_h(2, nc.sync)
        load_x(5)
        load_x(6)
        load_c(1)
        load_h(3, nc.sync)
        load_x(7)

        ident_f = keep.tile([P, P], F32, name="ident_f")
        make_identity(nc, ident_f[:])
        ident_b = keep.tile([P, P], BF16, name="ident_b")
        make_identity(nc, ident_b[:])
        warm = keep.tile([P, 1], F32, name="warm")
        nc.vector.memset(warm[:], 0.0)
        warm2 = keep.tile([P, 1], F32, name="warm2")
        nc.scalar.activation(out=warm2[:], in_=warm[:], func=ACT.Sigmoid)

        wg = keep.tile([P, 4 * G4], BF16, name="wg", align_bytes=64)
        wq = keep.tile([P, G4], U32, name="wq", align_bytes=64)
        ws = keep.tile([P, G4], U8, name="ws", align_bytes=64)
        xq = keep.tile([P, NT * P], U32, name="xq", align_bytes=64)
        xs = keep.tile([P, NT * P], U8, name="xs", align_bytes=64)
        hT_sb = [keep.tile([P, 4 * P], BF16, name="hT%d" % i) for i in range(4)]

        def w_regroup(g, on_scalar):
            dst = wg[:, g * 4 * U : (g + 1) * 4 * U].rearrange("p (c t) -> p c t", t=4)
            src = w_raw[g][:].rearrange("p (t c) -> p c t", t=4)
            if on_scalar:
                nc.scalar.copy(out=dst, in_=src)
            else:
                nc.vector.tensor_copy(out=dst, in_=src)

        def w_quant(g):
            nc.vector.quantize_mx(
                out=wq[:, g * U : (g + 1) * U].bitcast(FP8X4),
                scales=ws[:, g * U : (g + 1) * U],
                in_=wg[:, g * 4 * U : (g + 1) * 4 * U],
            )

        xt_of, xg_of, ht_of, mx_of, ms_of, ps_of, zt_of, a_of, c_of = {}, {}, {}, {}, {}, {}, {}, {}, {}

        def x_transpose(k):
            xt = psum.tile([P, 2, 2, P], F32, name="xt", tag="tz", bufs=6)
            xw = x_sb[k][:].bitcast(F32)
            for j in range(2):
                for u in range(2):
                    words = xw[:, j * (D // 2) + u : (j + 1) * (D // 2) : 2]
                    nc.tensor.transpose(xt[:, j, u, :], words, ident_f[:])
            xt_of[k] = xt

        def x_copy(k):
            xg = work.tile([P, 2 * D], BF16, name="xg", tag="xg", align_bytes=64)
            dst = xg[:].bitcast(F32).rearrange("p (j r u) -> p j r u", j=2, r=P, u=2)
            src = xt_of[k][:].rearrange("p j u r -> p j r u")
            if k in X_ON_SCALAR:
                nc.scalar.copy(out=dst, in_=src)
            else:
                nc.vector.tensor_copy(out=dst, in_=src)
            xg_of[k] = xg

        def x_quant(k):
            cols = slice(2 * k * P, (2 * k + 2) * P)
            nc.vector.quantize_mx(out=xq[:, cols].bitcast(FP8X4), scales=xs[:, cols], in_=xg_of[k][:])

        def h_transpose(i):
            ht = psum.tile([P, 4, P], BF16, name="ht", tag="tz", bufs=6)
            for j in range(4):
                nc.tensor.transpose(ht[:, j, :], ph_sb[i][:, j, :], ident_b[:])
            ht_of[i] = ht

        def h_copy(i):
            nc.scalar.copy(out=hT_sb[i][:], in_=ht_of[i][:].rearrange("p j r -> p (j r)"))

        def hT(t):
            return hT_sb[t // 4][:, (t % 4) * P : (t % 4 + 1) * P]

        def plain(k, j):
            z = psum.tile([P, G4], F32, name="z", tag="tz", bufs=6)
            nc.tensor.matmul(out=z[:], lhsT=hT(2 * k + j), rhs=u_sb[:], start=True, stop=False)
            zt_of[(k, j)] = z

        def plain_copy(k):
            z_sb = work.tile([P, 2, G4], F32, name="z_sb", tag="z_sb")
            for j in range(2):
                nc.scalar.copy(out=z_sb[:, j, :], in_=zt_of[(k, j)][:])
            ps_of[k] = z_sb

        def mx(k):
            banks = []
            if k in DIRECT:
                for j in range(2):
                    cols = slice((2 * k + j) * P, (2 * k + j + 1) * P)
                    m = psum.tile([P, G4], F32, name="m", tag="mt", bufs=2)
                    nc.tensor.matmul_mx(
                        out=m[:],
                        lhsT=xq[:, cols].bitcast(FP8X4),
                        lhsT_scale=xs[:, cols],
                        rhs=wq[:].bitcast(FP8X4),
                        rhs_scale=ws[:],
                        start=True,
                        stop=True,
                    )
                    banks.append(m)
            else:
                cols = slice(2 * k * P, (2 * k + 2) * P)
                for b in range(2):
                    mt = psum.tile([P, 2, 2 * P], F32, name="mt", tag="mt", bufs=2)
                    for gg in range(2):
                        g = 2 * b + gg
                        nc.tensor.matmul_mx(
                            out=mt[:, gg, :],
                            lhsT=wq[:, g * U : (g + 1) * U].bitcast(FP8X4),
                            lhsT_scale=ws[:, g * U : (g + 1) * U],
                            rhs=xq[:, cols].bitcast(FP8X4),
                            rhs_scale=xs[:, cols],
                            start=True,
                            stop=True,
                        )
                    banks.append(mt)
            mx_of[k] = banks

        def mx_out(k):
            if k in DIRECT:
                z_sb = ps_of[k]
                for j in range(2):
                    nc.vector.tensor_tensor(out=z_sb[:, j, :], in0=mx_of[k][j][:], in1=z_sb[:, j, :], op=ALU.add)
                return
            tiles = []
            for b in range(2):
                mt_sb = work.tile([P, 2, 2 * P], F32, name="mt_sb%d" % b, tag="mt_sb%d" % b)
                if b == 1 and k in M1_ON_SCALAR:
                    nc.scalar.copy(out=mt_sb[:], in_=mx_of[k][b][:])
                else:
                    nc.vector.tensor_copy(out=mt_sb[:], in_=mx_of[k][b][:])
                tiles.append(mt_sb)
            ms_of[k] = tiles

        def add_back(k):
            if k in DIRECT:
                return
            for j in range(2):
                for g in range(4):
                    nc.tensor.matmul(
                        out=zt_of[(k, j)][:, g * U : (g + 1) * U],
                        lhsT=ms_of[k][g // 2][:, g % 2, j * P : (j + 1) * P],
                        rhs=ident_f[:],
                        is_transpose=True,
                        start=False,
                        stop=(g == 3),
                    )

        def gates(k):
            a = work.tile([P, 2, G4], F32, name="a", tag="a")
            a_of[k] = a
            if k in DIRECT:
                z_sb = ps_of[k]
                nc.scalar.activation(out=a[:, :, 0 : 3 * U], in_=z_sb[:, :, 0 : 3 * U], func=ACT.Sigmoid)
                nc.scalar.activation(out=a[:, :, 3 * U : G4], in_=z_sb[:, :, 3 * U : G4], func=ACT.Tanh)
                return
            for j in range(2):
                z = zt_of[(k, j)]
                if k == NP - 1:
                    nc.scalar.activation(out=a[:, j, 0 : 2 * U], in_=z[:, 0 : 2 * U], func=ACT.Sigmoid)
                    nc.scalar.activation(out=a[:, j, 3 * U : G4], in_=z[:, 3 * U : G4], func=ACT.Tanh)
                    nc.scalar.activation(out=a[:, j, 2 * U : 3 * U], in_=z[:, 2 * U : 3 * U], func=ACT.Sigmoid)
                    continue
                nc.scalar.activation(out=a[:, j, 0 : 3 * U], in_=z[:, 0 : 3 * U], func=ACT.Sigmoid)
                nc.scalar.activation(out=a[:, j, 3 * U : G4], in_=z[:, 3 * U : G4], func=ACT.Tanh)

        def new_cell(k):
            fa = work.tile([P, 2, U], F32, name="fa", tag="fa")
            ib = work.tile([P, 2, U], F32, name="ib", tag="ib")
            c_sb = work.tile([P, 2, U], F32, name="c_sb", tag="c_sb")
            tc_sb = work.tile([P, 2, U], F32, name="tc_sb", tag="tc_sb")
            h_sb = work.tile([P, 2, U], F32, name="h_sb", tag="h_sb")
            c_of[k] = (fa, ib, c_sb, tc_sb, h_sb)

        ALL = slice(0, 2)

        def cell_mul(k, js=ALL):
            fa, ib = c_of[k][0], c_of[k][1]
            a = a_of[k]
            t0 = (2 * k) % 8
            pc = pc_sb[k // 4][:, t0 + js.start : t0 + js.stop, :]
            eng = nc.gpsimd if k in POOL_FA else nc.vector
            eng.tensor_tensor(out=fa[:, js], in0=a[:, js, U : 2 * U], in1=pc, op=ALU.mult)
            eng = nc.gpsimd if k in POOL_IB else nc.vector
            eng.tensor_tensor(out=ib[:, js], in0=a[:, js, 0:U], in1=a[:, js, 3 * U : G4], op=ALU.mult)

        def cell_add(k, js=ALL):
            fa, ib, c_sb = c_of[k][0], c_of[k][1], c_of[k][2]
            eng = nc.gpsimd if k in POOL_C else nc.vector
            eng.tensor_tensor(out=c_sb[:, js], in0=fa[:, js], in1=ib[:, js], op=ALU.add)
            nc.sync.dma_start(out=outv[1, :, 2 * k + js.start : 2 * k + js.stop, :], in_=c_sb[:, js])

        def cell_tanh(k, js=ALL):
            nc.scalar.activation(out=c_of[k][3][:, js], in_=c_of[k][2][:, js], func=ACT.Tanh)

        def hidden(k, js=ALL):
            tc_sb, h_sb = c_of[k][3], c_of[k][4]
            eng = nc.gpsimd if k in POOL_H else nc.vector
            eng.tensor_tensor(out=h_sb[:, js], in0=a_of[k][:, js, 2 * U : 3 * U], in1=tc_sb[:, js], op=ALU.mult)
            nc.sync.dma_start(out=outv[0, :, 2 * k + js.start : 2 * k + js.stop, :], in_=h_sb[:, js])

        x_transpose(0)
        h_transpose(0)
        x_copy(0)
        h_copy(0)
        w_regroup(0, False)
        w_regroup(1, False)
        w_quant(0)
        w_regroup(2, False)
        w_quant(1)
        x_quant(0)
        w_regroup(3, False)
        w_quant(2)
        x_transpose(1)
        w_quant(3)
        for s in range(-1, NP):
            if s + 2 < NP:
                x_copy(s + 2)
            if 0 <= s:
                plain(s, 0)
            if s + 1 < NP:
                mx(s + 1)
            if 0 <= s - 2 and s < NP - 1:
                cell_tanh(s - 2)
            if s + 1 < NP and s + 1 not in DIRECT:
                mx_out(s + 1)
            if 0 <= s:
                if s not in DIRECT:
                    plain(s, 1)
                    add_back(s)
                gates(s)
                new_cell(s)
            if s + 2 < NP:
                x_quant(s + 2)
            if s == NP - 1:
                break
            if 0 <= s - 2:
                hidden(s - 2)
            if 0 <= s - 1:
                cell_mul(s - 1)
                cell_add(s - 1)
            if s + 1 in DIRECT:
                mx_out(s + 1)
            if s + 3 < NP:
                x_transpose(s + 3)
            if s in (-1, 1, 3):
                h_transpose((s + 1) // 2 + 1)
                h_copy((s + 1) // 2 + 1)
        halves = (slice(0, 1), slice(1, 2))
        cell_tanh(NP - 3)
        for js in halves:
            cell_mul(NP - 2, js)
        cell_add(NP - 2)
        cell_tanh(NP - 2)
        for js in halves:
            cell_mul(NP - 1, js)
        for js in halves:
            cell_add(NP - 1, js)
            cell_tanh(NP - 1, js)
        hidden(NP - 3)
        hidden(NP - 2)
        for js in halves:
            hidden(NP - 1, js)
